import numpy as np
import ml_dtypes


def mxq(x, axis, fmt="e4m3"):
    dtype, down = {"e4m3": (ml_dtypes.float8_e4m3fn, 7), "e5m2": (ml_dtypes.float8_e5m2, 14)}[fmt]
    v = np.moveaxis(np.asarray(x, np.float32).astype(ml_dtypes.bfloat16).astype(np.float64), axis, -1)
    blocks = v.reshape(v.shape[:-1] + (-1, 32))
    amax = np.abs(blocks).max(-1, keepdims=True)
    byte = np.maximum(np.where(amax > 0, np.frexp(amax)[1] - 1 + 127, 0) - down, 1)
    scale = np.exp2(byte - 127.0)
    codes = (blocks / scale).astype(np.float32).astype(dtype).astype(np.float64)
    return np.moveaxis((codes * scale).reshape(v.shape), -1, axis)


WIDE = False


def mx_kscale(k):
    if not WIDE:
        return np.ones(k)
    levels = np.array([10, -10, 5, -5, 0])
    a = np.random.permutation(np.resize(levels, k // 512 * 4)).reshape(k // 512, 4)
    idx = np.arange(k)
    return np.exp2(a[idx // 512, idx % 128 // 32])


BF16 = ml_dtypes.bfloat16


def bf(x):
    return np.asarray(x, np.float32).astype(BF16)


def f64(x):
    return np.asarray(x).astype(np.float64)


B, N, D, HEAD, HALF = 4, 1024, 512, 1024, 512


def setup_inputs():
    t = mx_kscale(N)
    r = np.square(np.maximum(np.random.standard_normal((B, N, HALF)), 0.0))
    r = r / np.sqrt(np.sum(np.square(r), axis=-1, keepdims=True))
    return {"xr_n": bf(r / t[None, :, None]),
            "V": bf(np.random.standard_normal((N, N)) * 6.0 * np.sqrt(HALF / N) * t[:, None] * (t * t)[None, :])}


def reference(xr_n, V):
    xr = f64(xr_n)
    xq = mxq(xr, 2, "e4m3")
    cos = xq @ xq.transpose(0, 2, 1)
    weighted = f64(V)[None, :, :] * cos
    return mxq(weighted, 2, "e4m3") @ mxq(xr, 1, "e4m3")

@@ -1,0 +1,235 @@
+from contextlib import ExitStack
+
+import concourse.mybir as mybir
+from concourse.masks import make_identity
+
+BF16 = mybir.dt.bfloat16
+F32 = mybir.dt.float32
+U32 = mybir.dt.uint32
+U8 = mybir.dt.uint8
+FP8X4 = mybir.dt.float8_e4m3fn_x4
+
+P = 128
+PACK = 4
+PAIR = 2
+K_PASS = P * PACK
+BATCHES = 4
+POSITIONS = 1024
+FEATURES = 512
+HALVES = POSITIONS // K_PASS
+HALF_BATCHES = BATCHES * HALVES
+STEP_ROWS = PAIR * P
+STEPS_PER_BATCH = POSITIONS // STEP_ROWS
+STEPS = BATCHES * STEPS_PER_BATCH
+
+FLOPS = 2 * 2 * BATCHES * POSITIONS * POSITIONS * FEATURES
+
+
+def half_batch_in_stage(step, stage):
+    b, h = divmod(step - stage + STEPS_PER_BATCH, STEPS_PER_BATCH)
+    if h < HALVES and 1 <= b < BATCHES:
+        return HALVES * b + h
+    return None
+
+
+def tile_avey_pb_t_kernel(tc, xr_n, V, out):
+    nc = tc.nc
+    with ExitStack() as ctx:
+        resident = ctx.enter_context(tc.tile_pool(name="resident", bufs=1))
+        grouped_pool = ctx.enter_context(tc.tile_pool(name="grouped", bufs=2))
+        x_codes_pool = ctx.enter_context(tc.tile_pool(name="x_codes", bufs=4))
+        w_pool = ctx.enter_context(tc.tile_pool(name="weighted", bufs=3))
+        out_pool = ctx.enter_context(tc.tile_pool(name="out_rows", bufs=3))
+        flip_psum = ctx.enter_context(tc.psum_pool(name="flip_psum", bufs=2))
+        cos_psum = ctx.enter_context(tc.psum_pool(name="cos_psum", bufs=4))
+        acc_psum = ctx.enter_context(tc.psum_pool(name="acc_psum", bufs=2))
+
+        identity = resident.tile([P, P], F32, name="identity")
+        make_identity(nc, identity[:])
+
+        x_rows = {}
+        v_rows = {}
+        v_flipped = {}
+        feat_grouped = {}
+        feat_codes = {}
+        pos_grouped = {}
+        pos_codes = {}
+        w_grouped = {}
+        w_codes = {}
+
+        def load_x(j):
+            b, h = divmod(j, HALVES)
+            x_rows[j] = resident.tile([P, PACK, FEATURES], BF16, name="x_rows_%d" % j)
+            nc.sync.dma_start(
+                out=x_rows[j][:].rearrange("p (u e) f -> p u e f", e=PAIR),
+                in_=xr_n[b, h * K_PASS : (h + 1) * K_PASS, :].rearrange(
+                    "(u p e) f -> p u e f", p=P, e=PAIR
+                ),
+            )
+
+        def load_v(r):
+            v_rows[r] = resident.tile([P, PAIR, POSITIONS], BF16, name="v_rows_%d" % r)
+            nc.sync.dma_start(
+                out=v_rows[r][:],
+                in_=V[r * STEP_ROWS : (r + 1) * STEP_ROWS, :].rearrange("(p e) m -> p e m", e=PAIR),
+            )
+
+        def flip_two_blocks(words, grouped_words):
+            bank = flip_psum.tile([P, 2, PAIR, P], F32, name="flip_bank")
+            for k in range(2):
+                for u in range(PAIR):
+                    nc.tensor.transpose(
+                        bank[:, k, u, :], words[:, k, u * P : (u + 1) * P], identity[:]
+                    )
+            nc.scalar.copy(
+                out=grouped_words.rearrange("p (k c) u -> p k c u", k=2),
+                in_=bank[:].rearrange("p k u c -> p k c u"),
+            )
+
+        def flip_x(j):
+            feat_grouped[j] = grouped_pool.tile(
+                [P, K_PASS, PACK], BF16, name="feat_grouped", align_bytes=64
+            )
+            for u in range(PAIR):
+                flip_two_blocks(
+                    x_rows[j][:].bitcast(F32)[:, PAIR * u : PAIR * (u + 1), :],
+                    feat_grouped[j][:].bitcast(F32)[:, STEP_ROWS * u : STEP_ROWS * (u + 1), :],
+                )
+
+        def flip_v(r):
+            v_flipped[r] = resident.tile(
+                [P, HALVES, STEP_ROWS, PACK], BF16, name="v_flipped_%d" % r
+            )
+            words_per_pass = K_PASS // PAIR
+            for hm in range(HALVES):
+                flip_two_blocks(
+                    v_rows[r][:].bitcast(F32)[:, :, hm * words_per_pass : (hm + 1) * words_per_pass],
+                    v_flipped[r][:].bitcast(F32)[:, hm, :, :],
+                )
+
+        def quantise(pool, name, values):
+            codes = pool.tile([P, K_PASS], U32, name=name + "_codes", align_bytes=64)
+            scales = pool.tile([P, K_PASS], U8, name=name + "_scales", align_bytes=64)
+            nc.vector.quantize_mx(out=codes[:].bitcast(FP8X4), scales=scales[:], in_=values)
+            return codes, scales
+
+        def quantise_features(j):
+            feat_codes[j] = quantise(
+                x_codes_pool, "feat", feat_grouped[j][:].rearrange("p c t -> p (c t)")
+            )
+
+        def quantise_positions(j):
+            pos_codes[j] = quantise(
+                x_codes_pool, "pos", pos_grouped[j][:].rearrange("p f t -> p (f t)")
+            )
+
+        def regroup_positions(j, copy):
+            pos_grouped[j] = grouped_pool.tile(
+                [P, FEATURES, PACK], BF16, name="pos_grouped", align_bytes=64
+            )
+            copy(
+                out=pos_grouped[j][:].rearrange("p (c i) t -> p c t i", i=4),
+                in_=x_rows[j][:].rearrange("p t (c i) -> p c t i", i=4),
+            )
+
+        def weigh(step):
+            b, r = divmod(step, STEPS_PER_BATCH)
+            hn, u = divmod(r, PAIR)
+            n_codes, n_scales = feat_codes[HALVES * b + hn]
+            w_grouped[step] = w_pool.tile(
+                [P, HALVES, STEP_ROWS, PACK], BF16, name="w_grouped", align_bytes=64
+            )
+            for hm in range(HALVES):
+                m_codes, m_scales = feat_codes[HALVES * b + hm]
+                for e in range(PAIR):
+                    n_cols = slice((PAIR * u + e) * P, (PAIR * u + e + 1) * P)
+                    cos_bank = cos_psum.tile([P, PACK, P], F32, name="cos_bank")
+                    for t in range(PACK):
+                        m_cols = slice(t * P, (t + 1) * P)
+                        nc.tensor.matmul_mx(
+                            out=cos_bank[:, t, :],
+                            lhsT=m_codes[:, m_cols].bitcast(FP8X4),
+                            lhsT_scale=m_scales[:, m_cols],
+                            rhs=n_codes[:, n_cols].bitcast(FP8X4),
+                            rhs_scale=n_scales[:, n_cols],
+                            start=True,
+                            stop=True,
+                        )
+                    nc.vector.tensor_tensor(
+                        out=w_grouped[step][:, hm, e * P : (e + 1) * P, :],
+                        in0=cos_bank[:].rearrange("p t c -> p c t"),
+                        in1=v_flipped[r][:, hm, e * P : (e + 1) * P, :],
+                        op=mybir.AluOpType.mult,
+                    )
+
+        def quantise_weighted(step):
+            w_codes[step] = quantise(
+                w_pool, "w", w_grouped[step][:].rearrange("p h c t -> p (h c t)")
+            )
+
+        def second_product(step):
+            b, r = divmod(step, STEPS_PER_BATCH)
+            codes, scales = w_codes[step]
+            out_rows = out_pool.tile([P, PAIR, FEATURES], F32, name="out_rows")
+            for e in range(PAIR):
+                acc = acc_psum.tile([P, FEATURES], F32, name="acc")
+                for hm in range(HALVES):
+                    n_cols = slice(hm * STEP_ROWS + e * P, hm * STEP_ROWS + (e + 1) * P)
+                    x_codes, x_scales = pos_codes[HALVES * b + hm]
+                    nc.tensor.matmul_mx(
+                        out=acc[:],
+                        lhsT=codes[:, n_cols].bitcast(FP8X4),
+                        lhsT_scale=scales[:, n_cols],
+                        rhs=x_codes[:].bitcast(FP8X4),
+                        rhs_scale=x_scales[:],
+                        start=(hm == 0),
+                        stop=(hm == HALVES - 1),
+                    )
+                nc.scalar.copy(out=out_rows[:, e, :], in_=acc[:])
+            nc.sync.dma_start(
+                out=out[b, r * STEP_ROWS : (r + 1) * STEP_ROWS, :].rearrange(
+                    "(p e) f -> p e f", e=PAIR
+                ),
+                in_=out_rows[:],
+            )
+
+        with tc.manual_schedule():
+            load_x(0)
+            load_x(1)
+            load_v(0)
+            for r in range(1, STEPS_PER_BATCH):
+                load_v(r)
+                load_x(r + 1)
+            for j in range(STEPS_PER_BATCH + 1, HALF_BATCHES):
+                load_x(j)
+
+            for h in range(HALVES):
+                flip_x(h)
+                regroup_positions(h, nc.vector.tensor_copy)
+            flip_v(0)
+            for h in range(HALVES):
+                quantise_features(h)
+            for h in range(HALVES):
+                quantise_positions(h)
+
+            for step in range(STEPS + 1):
+                if step < STEPS:
+                    weigh(step)
+                if step + 1 < STEPS_PER_BATCH:
+                    flip_v(step + 1)
+                j = half_batch_in_stage(step, 0)
+                if j is not None:
+                    flip_x(j)
+                if step >= 1:
+                    second_product(step - 1)
+                j = half_batch_in_stage(step, 2)
+                if j is not None:
+                    regroup_positions(j, nc.scalar.copy)
+                j = half_batch_in_stage(step, 1)
+                if j is not None:
+                    quantise_features(j)
+                j = half_batch_in_stage(step, 3)
+                if j is not None:
+                    quantise_positions(j)
+                if step < STEPS:
+                    quantise_weighted(step)

@@ -38,8 +38,10 @@ def tile_avey_pb_t_kernel(tc, xr_n, V, out):
         resident = ctx.enter_context(tc.tile_pool(name="resident", bufs=1))
         grouped_pool = ctx.enter_context(tc.tile_pool(name="grouped", bufs=2))
         x_codes_pool = ctx.enter_context(tc.tile_pool(name="x_codes", bufs=4))
-        w_pool = ctx.enter_context(tc.tile_pool(name="weighted", bufs=3))
-        out_pool = ctx.enter_context(tc.tile_pool(name="out_rows", bufs=3))
+        w_pool = ctx.enter_context(tc.tile_pool(name="weighted", bufs=6))
+        detour_pool = ctx.enter_context(tc.tile_pool(name="detour", bufs=1))
+        w_codes_pool = ctx.enter_context(tc.tile_pool(name="w_codes", bufs=3))
+        out_pool = ctx.enter_context(tc.tile_pool(name="out_rows", bufs=4))
         flip_psum = ctx.enter_context(tc.psum_pool(name="flip_psum", bufs=2))
         cos_psum = ctx.enter_context(tc.psum_pool(name="cos_psum", bufs=4))
         acc_psum = ctx.enter_context(tc.psum_pool(name="acc_psum", bufs=2))
@@ -136,45 +138,63 @@ def tile_avey_pb_t_kernel(tc, xr_n, V, out):
             b, r = divmod(step, STEPS_PER_BATCH)
             hn, u = divmod(r, PAIR)
             n_codes, n_scales = feat_codes[HALVES * b + hn]
-            w_grouped[step] = w_pool.tile(
-                [P, HALVES, STEP_ROWS, PACK], BF16, name="w_grouped", align_bytes=64
-            )
-            for hm in range(HALVES):
+            w_grouped[step] = []
+            for bank in range(HALVES * PAIR):
+                hm, e = divmod(bank, PAIR)
                 m_codes, m_scales = feat_codes[HALVES * b + hm]
-                for e in range(PAIR):
-                    n_cols = slice((PAIR * u + e) * P, (PAIR * u + e + 1) * P)
-                    cos_bank = cos_psum.tile([P, PACK, P], F32, name="cos_bank")
-                    for t in range(PACK):
-                        m_cols = slice(t * P, (t + 1) * P)
-                        nc.tensor.matmul_mx(
-                            out=cos_bank[:, t, :],
-                            lhsT=m_codes[:, m_cols].bitcast(FP8X4),
-                            lhsT_scale=m_scales[:, m_cols],
-                            rhs=n_codes[:, n_cols].bitcast(FP8X4),
-                            rhs_scale=n_scales[:, n_cols],
-                            start=True,
-                            stop=True,
-                        )
+                n_cols = slice((PAIR * u + e) * P, (PAIR * u + e + 1) * P)
+                cos_bank = cos_psum.tile([P, PACK, P], F32, name="cos_bank")
+                for t in range(PACK):
+                    m_cols = slice(t * P, (t + 1) * P)
+                    nc.tensor.matmul_mx(
+                        out=cos_bank[:, t, :],
+                        lhsT=m_codes[:, m_cols].bitcast(FP8X4),
+                        lhsT_scale=m_scales[:, m_cols],
+                        rhs=n_codes[:, n_cols].bitcast(FP8X4),
+                        rhs_scale=n_scales[:, n_cols],
+                        start=True,
+                        stop=True,
+                    )
+                v_part = v_flipped[r][:, hm, e * P : (e + 1) * P, :]
+                if bank == 0:
+                    cos_copy = detour_pool.tile([P, P, PACK], F32, name="cos_copy")
+                    product = detour_pool.tile([P, P, PACK], BF16, name="w_detour", align_bytes=64)
+                    nc.scalar.copy(out=cos_copy[:], in_=cos_bank[:].rearrange("p t c -> p c t"))
+                    nc.gpsimd.tensor_tensor(
+                        out=product[:], in0=cos_copy[:], in1=v_part, op=mybir.AluOpType.mult
+                    )
+                else:
+                    product = w_pool.tile([P, P, PACK], BF16, name="w_direct", align_bytes=64)
                     nc.vector.tensor_tensor(
-                        out=w_grouped[step][:, hm, e * P : (e + 1) * P, :],
+                        out=product[:],
                         in0=cos_bank[:].rearrange("p t c -> p c t"),
-                        in1=v_flipped[r][:, hm, e * P : (e + 1) * P, :],
+                        in1=v_part,
                         op=mybir.AluOpType.mult,
                     )
+                w_grouped[step].append(product)
 
         def quantise_weighted(step):
-            w_codes[step] = quantise(
-                w_pool, "w", w_grouped[step][:].rearrange("p h c t -> p (h c t)")
-            )
+            codes = w_codes_pool.tile([P, K_PASS], U32, name="w_codes", align_bytes=64)
+            scales = w_codes_pool.tile([P, K_PASS], U8, name="w_scales", align_bytes=64)
+            for bank in (1, 2, 3, 0):
+                cols = slice(bank * P, (bank + 1) * P)
+                nc.vector.quantize_mx(
+                    out=codes[:, cols].bitcast(FP8X4),
+                    scales=scales[:, cols],
+                    in_=w_grouped[step][bank][:].rearrange("p c t -> p (c t)"),
+                )
+            w_codes[step] = (codes, scales)
 
         def second_product(step):
             b, r = divmod(step, STEPS_PER_BATCH)
             codes, scales = w_codes[step]
-            out_rows = out_pool.tile([P, PAIR, FEATURES], F32, name="out_rows")
+            rows = out[b, r * STEP_ROWS : (r + 1) * STEP_ROWS, :].rearrange(
+                "(p e) f -> p e f", e=PAIR
+            )
             for e in range(PAIR):
                 acc = acc_psum.tile([P, FEATURES], F32, name="acc")
                 for hm in range(HALVES):
-                    n_cols = slice(hm * STEP_ROWS + e * P, hm * STEP_ROWS + (e + 1) * P)
+                    n_cols = slice((PAIR * hm + e) * P, (PAIR * hm + e + 1) * P)
                     x_codes, x_scales = pos_codes[HALVES * b + hm]
                     nc.tensor.matmul_mx(
                         out=acc[:],
@@ -185,13 +205,9 @@ def tile_avey_pb_t_kernel(tc, xr_n, V, out):
                         start=(hm == 0),
                         stop=(hm == HALVES - 1),
                     )
-                nc.scalar.copy(out=out_rows[:, e, :], in_=acc[:])
-            nc.sync.dma_start(
-                out=out[b, r * STEP_ROWS : (r + 1) * STEP_ROWS, :].rearrange(
-                    "(p e) f -> p e f", e=PAIR
-                ),
-                in_=out_rows[:],
-            )
+                out_rows = out_pool.tile([P, FEATURES], F32, name="out_rows")
+                nc.scalar.copy(out=out_rows[:], in_=acc[:])
+                nc.sync.dma_start(out=rows[:, e, :], in_=out_rows[:])
 
         with tc.manual_schedule():
             load_x(0)
@@ -212,7 +228,7 @@ def tile_avey_pb_t_kernel(tc, xr_n, V, out):
             for h in range(HALVES):
                 quantise_positions(h)
 
-            for step in range(STEPS + 1):
+            for step in range(STEPS + 2):
                 if step < STEPS:
                     weigh(step)
                 if step + 1 < STEPS_PER_BATCH:
@@ -220,11 +236,11 @@ def tile_avey_pb_t_kernel(tc, xr_n, V, out):
                 j = half_batch_in_stage(step, 0)
                 if j is not None:
                     flip_x(j)
-                if step >= 1:
-                    second_product(step - 1)
+                if step >= 2:
+                    second_product(step - 2)
                 j = half_batch_in_stage(step, 2)
                 if j is not None:
-                    regroup_positions(j, nc.scalar.copy)
+                    regroup_positions(j, nc.vector.tensor_copy if j % HALVES == 0 else nc.scalar.copy)
                 j = half_batch_in_stage(step, 1)
                 if j is not None:
                     quantise_features(j)

@@ -176,7 +176,7 @@ def tile_avey_pb_t_kernel(tc, xr_n, V, out):
         def quantise_weighted(step):
             codes = w_codes_pool.tile([P, K_PASS], U32, name="w_codes", align_bytes=64)
             scales = w_codes_pool.tile([P, K_PASS], U8, name="w_scales", align_bytes=64)
-            for bank in (1, 2, 3, 0):
+            for bank in range(HALVES * PAIR):
                 cols = slice(bank * P, (bank + 1) * P)
                 nc.vector.quantize_mx(
                     out=codes[:, cols].bitcast(FP8X4),

@@ -21,30 +21,23 @@ HALF_BATCHES = BATCHES * HALVES
 STEP_ROWS = PAIR * P
 STEPS_PER_BATCH = POSITIONS // STEP_ROWS
 STEPS = BATCHES * STEPS_PER_BATCH
+DETOUR_BANK = 0
+QUANT_ORDER = (1, 3, 2, 0)
 
 FLOPS = 2 * 2 * BATCHES * POSITIONS * POSITIONS * FEATURES
-
-
-def half_batch_in_stage(step, stage):
-    b, h = divmod(step - stage + STEPS_PER_BATCH, STEPS_PER_BATCH)
-    if h < HALVES and 1 <= b < BATCHES:
-        return HALVES * b + h
-    return None
 
 
 def tile_avey_pb_t_kernel(tc, xr_n, V, out):
     nc = tc.nc
     with ExitStack() as ctx:
         resident = ctx.enter_context(tc.tile_pool(name="resident", bufs=1))
-        grouped_pool = ctx.enter_context(tc.tile_pool(name="grouped", bufs=2))
+        grouped_pool = ctx.enter_context(tc.tile_pool(name="grouped", bufs=4))
         x_codes_pool = ctx.enter_context(tc.tile_pool(name="x_codes", bufs=4))
         w_pool = ctx.enter_context(tc.tile_pool(name="weighted", bufs=6))
         detour_pool = ctx.enter_context(tc.tile_pool(name="detour", bufs=1))
         w_codes_pool = ctx.enter_context(tc.tile_pool(name="w_codes", bufs=3))
-        out_pool = ctx.enter_context(tc.tile_pool(name="out_rows", bufs=4))
-        flip_psum = ctx.enter_context(tc.psum_pool(name="flip_psum", bufs=2))
-        cos_psum = ctx.enter_context(tc.psum_pool(name="cos_psum", bufs=4))
-        acc_psum = ctx.enter_context(tc.psum_pool(name="acc_psum", bufs=2))
+        out_pool = ctx.enter_context(tc.tile_pool(name="out_rows", bufs=8))
+        banks = ctx.enter_context(tc.psum_pool(name="banks", bufs=8))
 
         identity = resident.tile([P, P], F32, name="identity")
         make_identity(nc, identity[:])
@@ -62,52 +55,61 @@ def tile_avey_pb_t_kernel(tc, xr_n, V, out):
         def load_x(j):
             b, h = divmod(j, HALVES)
             x_rows[j] = resident.tile([P, PACK, FEATURES], BF16, name="x_rows_%d" % j)
+            pieces = PAIR if b == 0 else 1
+            for i in range(pieces):
+                blocks = PACK // pieces
+                first_row = h * K_PASS + i * blocks * P
+                nc.sync.dma_start(
+                    out=x_rows[j][:, i * blocks : (i + 1) * blocks, :].rearrange(
+                        "p (u e) f -> p u e f", e=PAIR
+                    ),
+                    in_=xr_n[b, first_row : first_row + blocks * P, :].rearrange(
+                        "(u p e) f -> p u e f", p=P, e=PAIR
+                    ),
+                )
+
+        def load_v(r, hm):
+            v_rows[r, hm] = resident.tile([P, PAIR, K_PASS], BF16, name="v_rows_%d_%d" % (r, hm))
             nc.sync.dma_start(
-                out=x_rows[j][:].rearrange("p (u e) f -> p u e f", e=PAIR),
-                in_=xr_n[b, h * K_PASS : (h + 1) * K_PASS, :].rearrange(
-                    "(u p e) f -> p u e f", p=P, e=PAIR
-                ),
+                out=v_rows[r, hm][:],
+                in_=V[
+                    r * STEP_ROWS : (r + 1) * STEP_ROWS, hm * K_PASS : (hm + 1) * K_PASS
+                ].rearrange("(p e) m -> p e m", e=PAIR),
             )
 
-        def load_v(r):
-            v_rows[r] = resident.tile([P, PAIR, POSITIONS], BF16, name="v_rows_%d" % r)
-            nc.sync.dma_start(
-                out=v_rows[r][:],
-                in_=V[r * STEP_ROWS : (r + 1) * STEP_ROWS, :].rearrange("(p e) m -> p e m", e=PAIR),
-            )
-
-        def flip_two_blocks(words, grouped_words):
-            bank = flip_psum.tile([P, 2, PAIR, P], F32, name="flip_bank")
+        def flip_two_blocks(words, grouped_words, copy):
+            bank = banks.tile([P, 2, PAIR, P], F32, name="bank", tag="bank")
             for k in range(2):
                 for u in range(PAIR):
                     nc.tensor.transpose(
                         bank[:, k, u, :], words[:, k, u * P : (u + 1) * P], identity[:]
                     )
-            nc.scalar.copy(
+            copy(
                 out=grouped_words.rearrange("p (k c) u -> p k c u", k=2),
                 in_=bank[:].rearrange("p k u c -> p k c u"),
             )
 
-        def flip_x(j):
-            feat_grouped[j] = grouped_pool.tile(
-                [P, K_PASS, PACK], BF16, name="feat_grouped", align_bytes=64
-            )
-            for u in range(PAIR):
-                flip_two_blocks(
-                    x_rows[j][:].bitcast(F32)[:, PAIR * u : PAIR * (u + 1), :],
-                    feat_grouped[j][:].bitcast(F32)[:, STEP_ROWS * u : STEP_ROWS * (u + 1), :],
+        def flip_x(j, u, copy=nc.scalar.copy):
+            if u == 0:
+                feat_grouped[j] = grouped_pool.tile(
+                    [P, K_PASS, PACK], BF16, name="feat_grouped", align_bytes=64
                 )
+            flip_two_blocks(
+                x_rows[j][:].bitcast(F32)[:, PAIR * u : PAIR * (u + 1), :],
+                feat_grouped[j][:].bitcast(F32)[:, STEP_ROWS * u : STEP_ROWS * (u + 1), :],
+                copy,
+            )
 
-        def flip_v(r):
-            v_flipped[r] = resident.tile(
-                [P, HALVES, STEP_ROWS, PACK], BF16, name="v_flipped_%d" % r
-            )
-            words_per_pass = K_PASS // PAIR
-            for hm in range(HALVES):
-                flip_two_blocks(
-                    v_rows[r][:].bitcast(F32)[:, :, hm * words_per_pass : (hm + 1) * words_per_pass],
-                    v_flipped[r][:].bitcast(F32)[:, hm, :, :],
+        def flip_v(r, hm, copy=nc.scalar.copy):
+            if hm == 0:
+                v_flipped[r] = resident.tile(
+                    [P, HALVES, STEP_ROWS, PACK], BF16, name="v_flipped_%d" % r
                 )
+            flip_two_blocks(
+                v_rows[r, hm][:].bitcast(F32),
+                v_flipped[r][:].bitcast(F32)[:, hm, :, :],
+                copy,
+            )
 
         def quantise(pool, name, values):
             codes = pool.tile([P, K_PASS], U32, name=name + "_codes", align_bytes=64)
@@ -125,63 +127,64 @@ def tile_avey_pb_t_kernel(tc, xr_n, V, out):
                 x_codes_pool, "pos", pos_grouped[j][:].rearrange("p f t -> p (f t)")
             )
 
-        def regroup_positions(j, copy):
-            pos_grouped[j] = grouped_pool.tile(
-                [P, FEATURES, PACK], BF16, name="pos_grouped", align_bytes=64
-            )
+        def regroup_positions(j, copy, piece=0, pieces=1):
+            if piece == 0:
+                pos_grouped[j] = grouped_pool.tile(
+                    [P, FEATURES, PACK], BF16, name="pos_grouped", align_bytes=64
+                )
+            width = FEATURES // pieces
+            f = slice(piece * width, (piece + 1) * width)
             copy(
-                out=pos_grouped[j][:].rearrange("p (c i) t -> p c t i", i=4),
-                in_=x_rows[j][:].rearrange("p t (c i) -> p c t i", i=4),
+                out=pos_grouped[j][:, f, :].rearrange("p (c i) t -> p c t i", i=4),
+                in_=x_rows[j][:, :, f].rearrange("p t (c i) -> p c t i", i=4),
             )
 
-        def weigh(step):
+        def weigh(step, bank):
             b, r = divmod(step, STEPS_PER_BATCH)
             hn, u = divmod(r, PAIR)
             n_codes, n_scales = feat_codes[HALVES * b + hn]
-            w_grouped[step] = []
-            for bank in range(HALVES * PAIR):
-                hm, e = divmod(bank, PAIR)
-                m_codes, m_scales = feat_codes[HALVES * b + hm]
-                n_cols = slice((PAIR * u + e) * P, (PAIR * u + e + 1) * P)
-                cos_bank = cos_psum.tile([P, PACK, P], F32, name="cos_bank")
-                for t in range(PACK):
-                    m_cols = slice(t * P, (t + 1) * P)
-                    nc.tensor.matmul_mx(
-                        out=cos_bank[:, t, :],
-                        lhsT=m_codes[:, m_cols].bitcast(FP8X4),
-                        lhsT_scale=m_scales[:, m_cols],
-                        rhs=n_codes[:, n_cols].bitcast(FP8X4),
-                        rhs_scale=n_scales[:, n_cols],
-                        start=True,
-                        stop=True,
-                    )
-                v_part = v_flipped[r][:, hm, e * P : (e + 1) * P, :]
-                if bank == 0:
-                    cos_copy = detour_pool.tile([P, P, PACK], F32, name="cos_copy")
-                    product = detour_pool.tile([P, P, PACK], BF16, name="w_detour", align_bytes=64)
-                    nc.scalar.copy(out=cos_copy[:], in_=cos_bank[:].rearrange("p t c -> p c t"))
-                    nc.gpsimd.tensor_tensor(
-                        out=product[:], in0=cos_copy[:], in1=v_part, op=mybir.AluOpType.mult
-                    )
-                else:
-                    product = w_pool.tile([P, P, PACK], BF16, name="w_direct", align_bytes=64)
-                    nc.vector.tensor_tensor(
-                        out=product[:],
-                        in0=cos_bank[:].rearrange("p t c -> p c t"),
-                        in1=v_part,
-                        op=mybir.AluOpType.mult,
-                    )
-                w_grouped[step].append(product)
+            hm, e = divmod(bank, PAIR)
+            m_codes, m_scales = feat_codes[HALVES * b + hm]
+            n_cols = slice((PAIR * u + e) * P, (PAIR * u + e + 1) * P)
+            cos_bank = banks.tile([P, PACK, P], F32, name="bank", tag="bank")
+            for t in range(PACK):
+                m_cols = slice(t * P, (t + 1) * P)
+                nc.tensor.matmul_mx(
+                    out=cos_bank[:, t, :],
+                    lhsT=m_codes[:, m_cols].bitcast(FP8X4),
+                    lhsT_scale=m_scales[:, m_cols],
+                    rhs=n_codes[:, n_cols].bitcast(FP8X4),
+                    rhs_scale=n_scales[:, n_cols],
+                    start=True,
+                    stop=True,
+                )
+            v_part = v_flipped[r][:, hm, e * P : (e + 1) * P, :]
+            if bank == DETOUR_BANK:
+                cos_copy = detour_pool.tile([P, P, PACK], F32, name="cos_copy")
+                product = detour_pool.tile([P, P, PACK], BF16, name="w_detour", align_bytes=64)
+                nc.scalar.copy(out=cos_copy[:], in_=cos_bank[:].rearrange("p t c -> p c t"))
+                nc.gpsimd.tensor_tensor(
+                    out=product[:], in0=cos_copy[:], in1=v_part, op=mybir.AluOpType.mult
+                )
+            else:
+                product = w_pool.tile([P, P, PACK], BF16, name="w_direct", align_bytes=64)
+                nc.vector.tensor_tensor(
+                    out=product[:],
+                    in0=cos_bank[:].rearrange("p t c -> p c t"),
+                    in1=v_part,
+                    op=mybir.AluOpType.mult,
+                )
+            w_grouped[step, bank] = product
 
         def quantise_weighted(step):
             codes = w_codes_pool.tile([P, K_PASS], U32, name="w_codes", align_bytes=64)
             scales = w_codes_pool.tile([P, K_PASS], U8, name="w_scales", align_bytes=64)
-            for bank in range(HALVES * PAIR):
+            for bank in QUANT_ORDER:
                 cols = slice(bank * P, (bank + 1) * P)
                 nc.vector.quantize_mx(
                     out=codes[:, cols].bitcast(FP8X4),
                     scales=scales[:, cols],
-                    in_=w_grouped[step][bank][:].rearrange("p c t -> p (c t)"),
+                    in_=w_grouped[step, bank][:].rearrange("p c t -> p (c t)"),
                 )
             w_codes[step] = (codes, scales)
 
@@ -191,8 +194,8 @@ def tile_avey_pb_t_kernel(tc, xr_n, V, out):
             rows = out[b, r * STEP_ROWS : (r + 1) * STEP_ROWS, :].rearrange(
                 "(p e) f -> p e f", e=PAIR
             )
-            for e in range(PAIR):
-                acc = acc_psum.tile([P, FEATURES], F32, name="acc")
+            for e in (1, 0):
+                acc = banks.tile([P, FEATURES], F32, name="bank", tag="bank")
                 for hm in range(HALVES):
                     n_cols = slice((PAIR * hm + e) * P, (PAIR * hm + e + 1) * P)
                     x_codes, x_scales = pos_codes[HALVES * b + hm]
@@ -206,46 +209,63 @@ def tile_avey_pb_t_kernel(tc, xr_n, V, out):
                         stop=(hm == HALVES - 1),
                     )
                 out_rows = out_pool.tile([P, FEATURES], F32, name="out_rows")
-                nc.scalar.copy(out=out_rows[:], in_=acc[:])
-                nc.sync.dma_start(out=rows[:, e, :], in_=out_rows[:])
+                if step == STEPS - 1:
+                    hf = FEATURES // 2
+                    nc.scalar.copy(out=out_rows[:, :hf], in_=acc[:, :hf])
+                    nc.sync.dma_start(out=rows[:, e, :hf], in_=out_rows[:, :hf])
+                    out_rows2 = out_pool.tile([P, hf], F32, name="out_rows2")
+                    nc.vector.tensor_copy(out=out_rows2[:], in_=acc[:, hf:])
+                    nc.sync.dma_start(out=rows[:, e, hf:], in_=out_rows2[:])
+                else:
+                    nc.scalar.copy(out=out_rows[:], in_=acc[:])
+                    nc.sync.dma_start(out=rows[:, e, :], in_=out_rows[:])
 
         with tc.manual_schedule():
             load_x(0)
             load_x(1)
-            load_v(0)
+            load_v(0, 0)
+            load_v(0, 1)
             for r in range(1, STEPS_PER_BATCH):
-                load_v(r)
+                load_v(r, 0)
+                load_v(r, 1)
                 load_x(r + 1)
             for j in range(STEPS_PER_BATCH + 1, HALF_BATCHES):
                 load_x(j)
 
+            vcopy = nc.vector.tensor_copy
+            scopy = nc.scalar.copy
             for h in range(HALVES):
-                flip_x(h)
-                regroup_positions(h, nc.vector.tensor_copy)
-            flip_v(0)
+                for u in range(PAIR):
+                    flip_x(h, u)
+                regroup_positions(h, vcopy)
+            for hm in range(HALVES):
+                flip_v(0, hm)
             for h in range(HALVES):
                 quantise_features(h)
             for h in range(HALVES):
                 quantise_positions(h)
-
             for step in range(STEPS + 2):
+                b, r = divmod(step, STEPS_PER_BATCH)
+                nxt = HALVES * (b + 1)
                 if step < STEPS:
-                    weigh(step)
+                    for bank in range(HALVES * PAIR):
+                        weigh(step, bank)
                 if step + 1 < STEPS_PER_BATCH:
-                    flip_v(step + 1)
-                j = half_batch_in_stage(step, 0)
-                if j is not None:
-                    flip_x(j)
+                    flip_v(step + 1, 0)
+                    flip_v(step + 1, 1)
+                if b + 1 < BATCHES and 1 <= r <= 2:
+                    flip_x(nxt + r - 1, 0)
+                    flip_x(nxt + r - 1, 1)
                 if step >= 2:
                     second_product(step - 2)
-                j = half_batch_in_stage(step, 2)
-                if j is not None:
-                    regroup_positions(j, nc.vector.tensor_copy if j % HALVES == 0 else nc.scalar.copy)
-                j = half_batch_in_stage(step, 1)
-                if j is not None:
-                    quantise_features(j)
-                j = half_batch_in_stage(step, 3)
-                if j is not None:
-                    quantise_positions(j)
+                if b + 1 < BATCHES and r in (0, 3):
+                    regroup_positions(nxt, scopy, 1 if r else 0, 2)
+                if b + 1 < BATCHES:
+                    if r in (0, 2):
+                        regroup_positions(nxt + 1, vcopy, r // 2, 2)
+                if r < 2 and 0 < b < BATCHES:
+                    quantise_positions(HALVES * b + r)
+                if r >= 2 and b + 1 < BATCHES:
+                    quantise_features(nxt + r - 2)
                 if step < STEPS:
                     quantise_weighted(step)

@@ -21,8 +21,7 @@ HALF_BATCHES = BATCHES * HALVES
 STEP_ROWS = PAIR * P
 STEPS_PER_BATCH = POSITIONS // STEP_ROWS
 STEPS = BATCHES * STEPS_PER_BATCH
-DETOUR_BANK = 0
-QUANT_ORDER = (1, 3, 2, 0)
+
 
 FLOPS = 2 * 2 * BATCHES * POSITIONS * POSITIONS * FEATURES
 
@@ -34,7 +33,6 @@ def tile_avey_pb_t_kernel(tc, xr_n, V, out):
         grouped_pool = ctx.enter_context(tc.tile_pool(name="grouped", bufs=4))
         x_codes_pool = ctx.enter_context(tc.tile_pool(name="x_codes", bufs=4))
         w_pool = ctx.enter_context(tc.tile_pool(name="weighted", bufs=6))
-        detour_pool = ctx.enter_context(tc.tile_pool(name="detour", bufs=1))
         w_codes_pool = ctx.enter_context(tc.tile_pool(name="w_codes", bufs=3))
         out_pool = ctx.enter_context(tc.tile_pool(name="out_rows", bufs=8))
         banks = ctx.enter_context(tc.psum_pool(name="banks", bufs=8))
@@ -143,7 +141,7 @@ def tile_avey_pb_t_kernel(tc, xr_n, V, out):
             b, r = divmod(step, STEPS_PER_BATCH)
             hn, u = divmod(r, PAIR)
             n_codes, n_scales = feat_codes[HALVES * b + hn]
-            hm, e = divmod(bank, PAIR)
+            e, hm = divmod(bank, HALVES)
             m_codes, m_scales = feat_codes[HALVES * b + hm]
             n_cols = slice((PAIR * u + e) * P, (PAIR * u + e + 1) * P)
             cos_bank = banks.tile([P, PACK, P], F32, name="bank", tag="bank")
@@ -159,32 +157,24 @@ def tile_avey_pb_t_kernel(tc, xr_n, V, out):
                     stop=True,
                 )
             v_part = v_flipped[r][:, hm, e * P : (e + 1) * P, :]
-            if bank == DETOUR_BANK:
-                cos_copy = detour_pool.tile([P, P, PACK], F32, name="cos_copy")
-                product = detour_pool.tile([P, P, PACK], BF16, name="w_detour", align_bytes=64)
-                nc.scalar.copy(out=cos_copy[:], in_=cos_bank[:].rearrange("p t c -> p c t"))
-                nc.gpsimd.tensor_tensor(
-                    out=product[:], in0=cos_copy[:], in1=v_part, op=mybir.AluOpType.mult
-                )
-            else:
-                product = w_pool.tile([P, P, PACK], BF16, name="w_direct", align_bytes=64)
-                nc.vector.tensor_tensor(
-                    out=product[:],
-                    in0=cos_bank[:].rearrange("p t c -> p c t"),
-                    in1=v_part,
-                    op=mybir.AluOpType.mult,
-                )
-            w_grouped[step, bank] = product
+            if hm == 0:
+                w_grouped[step, e] = w_pool.tile([P, HALVES, P, PACK], BF16, name="w_grouped", align_bytes=64)
+            nc.vector.tensor_tensor(
+                out=w_grouped[step, e][:, hm, :, :],
+                in0=cos_bank[:].rearrange("p t c -> p c t"),
+                in1=v_part,
+                op=mybir.AluOpType.mult,
+            )
 
         def quantise_weighted(step):
             codes = w_codes_pool.tile([P, K_PASS], U32, name="w_codes", align_bytes=64)
             scales = w_codes_pool.tile([P, K_PASS], U8, name="w_scales", align_bytes=64)
-            for bank in QUANT_ORDER:
-                cols = slice(bank * P, (bank + 1) * P)
+            for e in range(PAIR):
+                cols = slice(e * HALVES * P, (e + 1) * HALVES * P)
                 nc.vector.quantize_mx(
                     out=codes[:, cols].bitcast(FP8X4),
                     scales=scales[:, cols],
-                    in_=w_grouped[step, bank][:].rearrange("p c t -> p (c t)"),
+                    in_=w_grouped[step, e][:].rearrange("p h c t -> p (h c t)"),
                 )
             w_codes[step] = (codes, scales)
 
@@ -194,10 +184,10 @@ def tile_avey_pb_t_kernel(tc, xr_n, V, out):
             rows = out[b, r * STEP_ROWS : (r + 1) * STEP_ROWS, :].rearrange(
                 "(p e) f -> p e f", e=PAIR
             )
-            for e in (1, 0):
+            for e in range(PAIR):
                 acc = banks.tile([P, FEATURES], F32, name="bank", tag="bank")
                 for hm in range(HALVES):
-                    n_cols = slice((PAIR * hm + e) * P, (PAIR * hm + e + 1) * P)
+                    n_cols = slice((HALVES * e + hm) * P, (HALVES * e + hm + 1) * P)
                     x_codes, x_scales = pos_codes[HALVES * b + hm]
                     nc.tensor.matmul_mx(
                         out=acc[:],
@@ -258,11 +248,8 @@ def tile_avey_pb_t_kernel(tc, xr_n, V, out):
                     flip_x(nxt + r - 1, 1)
                 if step >= 2:
                     second_product(step - 2)
-                if b + 1 < BATCHES and r in (0, 3):
-                    regroup_positions(nxt, scopy, 1 if r else 0, 2)
                 if b + 1 < BATCHES:
-                    if r in (0, 2):
-                        regroup_positions(nxt + 1, vcopy, r // 2, 2)
+                    regroup_positions(nxt + r // 2, scopy, r % 2, 2)
                 if r < 2 and 0 < b < BATCHES:
                     quantise_positions(HALVES * b + r)
                 if r >= 2 and b + 1 < BATCHES:

@@ -21,6 +21,10 @@ HALF_BATCHES = BATCHES * HALVES
 STEP_ROWS = PAIR * P
 STEPS_PER_BATCH = POSITIONS // STEP_ROWS
 STEPS = BATCHES * STEPS_PER_BATCH
+DETOUR_COLS = 96
+FIRST_DETOUR = 1
+BANK_ORDER = (0, 2, 3, 1)
+W_BUFS = (1, 2)
 
 
 FLOPS = 2 * 2 * BATCHES * POSITIONS * POSITIONS * FEATURES
@@ -34,6 +38,7 @@ def tile_avey_pb_t_kernel(tc, xr_n, V, out):
         x_codes_pool = ctx.enter_context(tc.tile_pool(name="x_codes", bufs=4))
         w_pool = ctx.enter_context(tc.tile_pool(name="weighted", bufs=6))
         w_codes_pool = ctx.enter_context(tc.tile_pool(name="w_codes", bufs=3))
+        detour_pool = ctx.enter_context(tc.tile_pool(name="detour", bufs=2))
         out_pool = ctx.enter_context(tc.tile_pool(name="out_rows", bufs=8))
         banks = ctx.enter_context(tc.psum_pool(name="banks", bufs=8))
 
@@ -49,6 +54,8 @@ def tile_avey_pb_t_kernel(tc, xr_n, V, out):
         pos_codes = {}
         w_grouped = {}
         w_codes = {}
+        cos_banks = {}
+        cos_copies = {}
 
         def load_x(j):
             b, h = divmod(j, HALVES)
@@ -137,7 +144,7 @@ def tile_avey_pb_t_kernel(tc, xr_n, V, out):
                 in_=x_rows[j][:, :, f].rearrange("p t (c i) -> p c t i", i=4),
             )
 
-        def weigh(step, bank):
+        def fill_bank(step, bank):
             b, r = divmod(step, STEPS_PER_BATCH)
             hn, u = divmod(r, PAIR)
             n_codes, n_scales = feat_codes[HALVES * b + hn]
@@ -156,20 +163,50 @@ def tile_avey_pb_t_kernel(tc, xr_n, V, out):
                     start=True,
                     stop=True,
                 )
+            cos_banks[step, bank] = cos_bank
+
+        def detour_cols(step, bank):
+            return DETOUR_COLS if bank == 0 and step >= FIRST_DETOUR else 0
+
+        def copy_for_detour(step, bank):
+            split = detour_cols(step, bank)
+            if split:
+                cos_copies[step] = detour_pool.tile([P, split, PACK], F32, name="cos_copy")
+                nc.scalar.copy(
+                    out=cos_copies[step][:],
+                    in_=cos_banks[step, bank][:].rearrange("p t c -> p c t")[:, :split, :],
+                )
+
+        def weigh(step, bank):
+            r = step % STEPS_PER_BATCH
+            e, hm = divmod(bank, HALVES)
             v_part = v_flipped[r][:, hm, e * P : (e + 1) * P, :]
             if hm == 0:
-                w_grouped[step, e] = w_pool.tile([P, HALVES, P, PACK], BF16, name="w_grouped", align_bytes=64)
-            nc.vector.tensor_tensor(
-                out=w_grouped[step, e][:, hm, :, :],
-                in0=cos_bank[:].rearrange("p t c -> p c t"),
-                in1=v_part,
-                op=mybir.AluOpType.mult,
-            )
+                w_grouped[step, e] = w_pool.tile(
+                    [P, HALVES, P, PACK], BF16, name="w_grouped_%d" % e, align_bytes=64, bufs=W_BUFS[e]
+                )
+            product = w_grouped[step, e][:, hm, :, :]
+            cos = cos_banks[step, bank][:].rearrange("p t c -> p c t")
+            split = detour_cols(step, bank)
+            if split:
+                nc.gpsimd.tensor_tensor(
+                    out=product[:, :split, :],
+                    in0=cos_copies[step][:],
+                    in1=v_part[:, :split, :],
+                    op=mybir.AluOpType.mult,
+                )
+            if split < P:
+                nc.vector.tensor_tensor(
+                    out=product[:, split:, :],
+                    in0=cos[:, split:, :],
+                    in1=v_part[:, split:, :],
+                    op=mybir.AluOpType.mult,
+                )
 
         def quantise_weighted(step):
             codes = w_codes_pool.tile([P, K_PASS], U32, name="w_codes", align_bytes=64)
             scales = w_codes_pool.tile([P, K_PASS], U8, name="w_scales", align_bytes=64)
-            for e in range(PAIR):
+            for e in (1, 0):
                 cols = slice(e * HALVES * P, (e + 1) * HALVES * P)
                 nc.vector.quantize_mx(
                     out=codes[:, cols].bitcast(FP8X4),
@@ -184,7 +221,7 @@ def tile_avey_pb_t_kernel(tc, xr_n, V, out):
             rows = out[b, r * STEP_ROWS : (r + 1) * STEP_ROWS, :].rearrange(
                 "(p e) f -> p e f", e=PAIR
             )
-            for e in range(PAIR):
+            for e in (1, 0):
                 acc = banks.tile([P, FEATURES], F32, name="bank", tag="bank")
                 for hm in range(HALVES):
                     n_cols = slice((HALVES * e + hm) * P, (HALVES * e + hm + 1) * P)
@@ -238,8 +275,13 @@ def tile_avey_pb_t_kernel(tc, xr_n, V, out):
                 b, r = divmod(step, STEPS_PER_BATCH)
                 nxt = HALVES * (b + 1)
                 if step < STEPS:
-                    for bank in range(HALVES * PAIR):
+                    for bank in BANK_ORDER:
+                        if bank > 0 or step == 0:
+                            fill_bank(step, bank)
                         weigh(step, bank)
+                if step + 1 < STEPS:
+                    fill_bank(step + 1, 0)
+                    copy_for_detour(step + 1, 0)
                 if step + 1 < STEPS_PER_BATCH:
                     flip_v(step + 1, 0)
                     flip_v(step + 1, 1)

@@ -21,7 +21,7 @@ HALF_BATCHES = BATCHES * HALVES
 STEP_ROWS = PAIR * P
 STEPS_PER_BATCH = POSITIONS // STEP_ROWS
 STEPS = BATCHES * STEPS_PER_BATCH
-DETOUR_COLS = 96
+DETOUR_COLS = 128
 FIRST_DETOUR = 1
 BANK_ORDER = (0, 2, 3, 1)
 W_BUFS = (1, 2)
@@ -291,7 +291,10 @@ def tile_avey_pb_t_kernel(tc, xr_n, V, out):
                 if step >= 2:
                     second_product(step - 2)
                 if b + 1 < BATCHES:
-                    regroup_positions(nxt + r // 2, scopy, r % 2, 2)
+                    if r in (0, 3):
+                        regroup_positions(nxt, scopy, 1 if r else 0, 2)
+                    if r in (0, 2):
+                        regroup_positions(nxt + 1, vcopy, r // 2, 2)
                 if r < 2 and 0 < b < BATCHES:
                     quantise_positions(HALVES * b + r)
                 if r >= 2 and b + 1 < BATCHES:

@@ -132,17 +132,23 @@ def tile_avey_pb_t_kernel(tc, xr_n, V, out):
                 x_codes_pool, "pos", pos_grouped[j][:].rearrange("p f t -> p (f t)")
             )
 
-        def regroup_positions(j, copy, piece=0, pieces=1):
+        def regroup_positions(j, copy, piece=0, pieces=1, run=4):
             if piece == 0:
                 pos_grouped[j] = grouped_pool.tile(
                     [P, FEATURES, PACK], BF16, name="pos_grouped", align_bytes=64
                 )
             width = FEATURES // pieces
             f = slice(piece * width, (piece + 1) * width)
-            copy(
-                out=pos_grouped[j][:, f, :].rearrange("p (c i) t -> p c t i", i=4),
-                in_=x_rows[j][:, :, f].rearrange("p t (c i) -> p c t i", i=4),
-            )
+            if run == 1:
+                copy(
+                    out=pos_grouped[j][:, f, :],
+                    in_=x_rows[j][:, :, f].rearrange("p t f -> p f t"),
+                )
+            else:
+                copy(
+                    out=pos_grouped[j][:, f, :].rearrange("p (c i) t -> p c t i", i=run),
+                    in_=x_rows[j][:, :, f].rearrange("p t (c i) -> p c t i", i=run),
+                )
 
         def fill_bank(step, bank):
             b, r = divmod(step, STEPS_PER_BATCH)
@@ -292,7 +298,7 @@ def tile_avey_pb_t_kernel(tc, xr_n, V, out):
                     second_product(step - 2)
                 if b + 1 < BATCHES:
                     if r in (0, 3):
-                        regroup_positions(nxt, scopy, 1 if r else 0, 2)
+                        regroup_positions(nxt, scopy, 1 if r else 0, 2, run=1)
                     if r in (0, 2):
                         regroup_positions(nxt + 1, vcopy, r // 2, 2)
                 if r < 2 and 0 < b < BATCHES:

@@ -297,10 +297,10 @@ def tile_avey_pb_t_kernel(tc, xr_n, V, out):
                 if step >= 2:
                     second_product(step - 2)
                 if b + 1 < BATCHES:
-                    if r in (0, 3):
-                        regroup_positions(nxt, scopy, 1 if r else 0, 2, run=1)
-                    if r in (0, 2):
-                        regroup_positions(nxt + 1, vcopy, r // 2, 2)
+                    if r in (1, 2) if b == 0 else r == 1:
+                        regroup_positions(nxt + r // 2, vcopy, r % 2, 2)
+                    else:
+                        regroup_positions(nxt + r // 2, scopy, r % 2, 2, run=1)
                 if r < 2 and 0 < b < BATCHES:
                     quantise_positions(HALVES * b + r)
                 if r >= 2 and b + 1 < BATCHES:

@@ -23,7 +23,7 @@ STEPS_PER_BATCH = POSITIONS // STEP_ROWS
 STEPS = BATCHES * STEPS_PER_BATCH
 DETOUR_COLS = 128
 FIRST_DETOUR = 1
-BANK_ORDER = (0, 2, 3, 1)
+BANK_ORDER = (0, 2, 1, 3)
 W_BUFS = (1, 2)
 
 
@@ -212,13 +212,18 @@ def tile_avey_pb_t_kernel(tc, xr_n, V, out):
         def quantise_weighted(step):
             codes = w_codes_pool.tile([P, K_PASS], U32, name="w_codes", align_bytes=64)
             scales = w_codes_pool.tile([P, K_PASS], U8, name="w_scales", align_bytes=64)
-            for e in (1, 0):
-                cols = slice(e * HALVES * P, (e + 1) * HALVES * P)
-                nc.vector.quantize_mx(
-                    out=codes[:, cols].bitcast(FP8X4),
-                    scales=scales[:, cols],
-                    in_=w_grouped[step, e][:].rearrange("p h c t -> p (h c t)"),
-                )
+            for e in (0, 1):
+                parts = HALVES if step == STEPS - 1 else 1
+                n = HALVES // parts
+                for i in range(parts):
+                    cols = slice((e * HALVES + i * n) * P, (e * HALVES + (i + 1) * n) * P)
+                    nc.vector.quantize_mx(
+                        out=codes[:, cols].bitcast(FP8X4),
+                        scales=scales[:, cols],
+                        in_=w_grouped[step, e][:, i * n : (i + 1) * n, :, :].rearrange(
+                            "p h c t -> p (h c t)"
+                        ),
+                    )
             w_codes[step] = (codes, scales)
 
         def second_product(step):
@@ -227,7 +232,7 @@ def tile_avey_pb_t_kernel(tc, xr_n, V, out):
             rows = out[b, r * STEP_ROWS : (r + 1) * STEP_ROWS, :].rearrange(
                 "(p e) f -> p e f", e=PAIR
             )
-            for e in (1, 0):
+            for e in (0, 1):
                 acc = banks.tile([P, FEATURES], F32, name="bank", tag="bank")
                 for hm in range(HALVES):
                     n_cols = slice((HALVES * e + hm) * P, (HALVES * e + hm + 1) * P)

from contextlib import ExitStack

import concourse.mybir as mybir
from concourse.masks import make_identity

BF16 = mybir.dt.bfloat16
F32 = mybir.dt.float32
U32 = mybir.dt.uint32
U8 = mybir.dt.uint8
FP8X4 = mybir.dt.float8_e4m3fn_x4

P = 128
PACK = 4
PAIR = 2
K_PASS = P * PACK
BATCHES = 4
POSITIONS = 1024
FEATURES = 512
HALVES = POSITIONS // K_PASS
HALF_BATCHES = BATCHES * HALVES
STEP_ROWS = PAIR * P
STEPS_PER_BATCH = POSITIONS // STEP_ROWS
STEPS = BATCHES * STEPS_PER_BATCH
DETOUR_COLS = 128
FIRST_DETOUR = 1
BANK_ORDER = (0, 2, 1, 3)
W_BUFS = (1, 2)


FLOPS = 2 * 2 * BATCHES * POSITIONS * POSITIONS * FEATURES


def tile_avey_pb_t_kernel(tc, xr_n, V, out):
    nc = tc.nc
    with ExitStack() as ctx:
        resident = ctx.enter_context(tc.tile_pool(name="resident", bufs=1))
        grouped_pool = ctx.enter_context(tc.tile_pool(name="grouped", bufs=4))
        x_codes_pool = ctx.enter_context(tc.tile_pool(name="x_codes", bufs=4))
        w_pool = ctx.enter_context(tc.tile_pool(name="weighted", bufs=6))
        w_codes_pool = ctx.enter_context(tc.tile_pool(name="w_codes", bufs=3))
        detour_pool = ctx.enter_context(tc.tile_pool(name="detour", bufs=2))
        out_pool = ctx.enter_context(tc.tile_pool(name="out_rows", bufs=8))
        banks = ctx.enter_context(tc.psum_pool(name="banks", bufs=8))

        identity = resident.tile([P, P], F32, name="identity")
        make_identity(nc, identity[:])

        x_rows = {}
        v_rows = {}
        v_flipped = {}
        feat_grouped = {}
        feat_codes = {}
        pos_grouped = {}
        pos_codes = {}
        w_grouped = {}
        w_codes = {}
        cos_banks = {}
        cos_copies = {}

        def load_x(j):
            b, h = divmod(j, HALVES)
            x_rows[j] = resident.tile([P, PACK, FEATURES], BF16, name="x_rows_%d" % j)
            pieces = PAIR if b == 0 else 1
            for i in range(pieces):
                blocks = PACK // pieces
                first_row = h * K_PASS + i * blocks * P
                nc.sync.dma_start(
                    out=x_rows[j][:, i * blocks : (i + 1) * blocks, :].rearrange(
                        "p (u e) f -> p u e f", e=PAIR
                    ),
                    in_=xr_n[b, first_row : first_row + blocks * P, :].rearrange(
                        "(u p e) f -> p u e f", p=P, e=PAIR
                    ),
                )

        def load_v(r, hm):
            v_rows[r, hm] = resident.tile([P, PAIR, K_PASS], BF16, name="v_rows_%d_%d" % (r, hm))
            nc.sync.dma_start(
                out=v_rows[r, hm][:],
                in_=V[
                    r * STEP_ROWS : (r + 1) * STEP_ROWS, hm * K_PASS : (hm + 1) * K_PASS
                ].rearrange("(p e) m -> p e m", e=PAIR),
            )

        def flip_two_blocks(words, grouped_words, copy):
            bank = banks.tile([P, 2, PAIR, P], F32, name="bank", tag="bank")
            for k in range(2):
                for u in range(PAIR):
                    nc.tensor.transpose(
                        bank[:, k, u, :], words[:, k, u * P : (u + 1) * P], identity[:]
                    )
            copy(
                out=grouped_words.rearrange("p (k c) u -> p k c u", k=2),
                in_=bank[:].rearrange("p k u c -> p k c u"),
            )

        def flip_x(j, u, copy=nc.scalar.copy):
            if u == 0:
                feat_grouped[j] = grouped_pool.tile(
                    [P, K_PASS, PACK], BF16, name="feat_grouped", align_bytes=64
                )
            flip_two_blocks(
                x_rows[j][:].bitcast(F32)[:, PAIR * u : PAIR * (u + 1), :],
                feat_grouped[j][:].bitcast(F32)[:, STEP_ROWS * u : STEP_ROWS * (u + 1), :],
                copy,
            )

        def flip_v(r, hm, copy=nc.scalar.copy):
            if hm == 0:
                v_flipped[r] = resident.tile(
                    [P, HALVES, STEP_ROWS, PACK], BF16, name="v_flipped_%d" % r
                )
            flip_two_blocks(
                v_rows[r, hm][:].bitcast(F32),
                v_flipped[r][:].bitcast(F32)[:, hm, :, :],
                copy,
            )

        def quantise(pool, name, values):
            codes = pool.tile([P, K_PASS], U32, name=name + "_codes", align_bytes=64)
            scales = pool.tile([P, K_PASS], U8, name=name + "_scales", align_bytes=64)
            nc.vector.quantize_mx(out=codes[:].bitcast(FP8X4), scales=scales[:], in_=values)
            return codes, scales

        def quantise_features(j):
            feat_codes[j] = quantise(
                x_codes_pool, "feat", feat_grouped[j][:].rearrange("p c t -> p (c t)")
            )

        def quantise_positions(j):
            pos_codes[j] = quantise(
                x_codes_pool, "pos", pos_grouped[j][:].rearrange("p f t -> p (f t)")
            )

        def regroup_positions(j, copy, piece=0, pieces=1, run=4):
            if piece == 0:
                pos_grouped[j] = grouped_pool.tile(
                    [P, FEATURES, PACK], BF16, name="pos_grouped", align_bytes=64
                )
            width = FEATURES // pieces
            f = slice(piece * width, (piece + 1) * width)
            if run == 1:
                copy(
                    out=pos_grouped[j][:, f, :],
                    in_=x_rows[j][:, :, f].rearrange("p t f -> p f t"),
                )
            else:
                copy(
                    out=pos_grouped[j][:, f, :].rearrange("p (c i) t -> p c t i", i=run),
                    in_=x_rows[j][:, :, f].rearrange("p t (c i) -> p c t i", i=run),
                )

        def fill_bank(step, bank):
            b, r = divmod(step, STEPS_PER_BATCH)
            hn, u = divmod(r, PAIR)
            n_codes, n_scales = feat_codes[HALVES * b + hn]
            e, hm = divmod(bank, HALVES)
            m_codes, m_scales = feat_codes[HALVES * b + hm]
            n_cols = slice((PAIR * u + e) * P, (PAIR * u + e + 1) * P)
            cos_bank = banks.tile([P, PACK, P], F32, name="bank", tag="bank")
            for t in range(PACK):
                m_cols = slice(t * P, (t + 1) * P)
                nc.tensor.matmul_mx(
                    out=cos_bank[:, t, :],
                    lhsT=m_codes[:, m_cols].bitcast(FP8X4),
                    lhsT_scale=m_scales[:, m_cols],
                    rhs=n_codes[:, n_cols].bitcast(FP8X4),
                    rhs_scale=n_scales[:, n_cols],
                    start=True,
                    stop=True,
                )
            cos_banks[step, bank] = cos_bank

        def detour_cols(step, bank):
            return DETOUR_COLS if bank == 0 and step >= FIRST_DETOUR else 0

        def copy_for_detour(step, bank):
            split = detour_cols(step, bank)
            if split:
                cos_copies[step] = detour_pool.tile([P, split, PACK], F32, name="cos_copy")
                nc.scalar.copy(
                    out=cos_copies[step][:],
                    in_=cos_banks[step, bank][:].rearrange("p t c -> p c t")[:, :split, :],
                )

        def weigh(step, bank):
            r = step % STEPS_PER_BATCH
            e, hm = divmod(bank, HALVES)
            v_part = v_flipped[r][:, hm, e * P : (e + 1) * P, :]
            if hm == 0:
                w_grouped[step, e] = w_pool.tile(
                    [P, HALVES, P, PACK], BF16, name="w_grouped_%d" % e, align_bytes=64, bufs=W_BUFS[e]
                )
            product = w_grouped[step, e][:, hm, :, :]
            cos = cos_banks[step, bank][:].rearrange("p t c -> p c t")
            split = detour_cols(step, bank)
            if split:
                nc.gpsimd.tensor_tensor(
                    out=product[:, :split, :],
                    in0=cos_copies[step][:],
                    in1=v_part[:, :split, :],
                    op=mybir.AluOpType.mult,
                )
            if split < P:
                nc.vector.tensor_tensor(
                    out=product[:, split:, :],
                    in0=cos[:, split:, :],
                    in1=v_part[:, split:, :],
                    op=mybir.AluOpType.mult,
                )

        def quantise_weighted(step):
            codes = w_codes_pool.tile([P, K_PASS], U32, name="w_codes", align_bytes=64)
            scales = w_codes_pool.tile([P, K_PASS], U8, name="w_scales", align_bytes=64)
            for e in (0, 1):
                parts = HALVES if step == STEPS - 1 else 1
                n = HALVES // parts
                for i in range(parts):
                    cols = slice((e * HALVES + i * n) * P, (e * HALVES + (i + 1) * n) * P)
                    nc.vector.quantize_mx(
                        out=codes[:, cols].bitcast(FP8X4),
                        scales=scales[:, cols],
                        in_=w_grouped[step, e][:, i * n : (i + 1) * n, :, :].rearrange(
                            "p h c t -> p (h c t)"
                        ),
                    )
            w_codes[step] = (codes, scales)

        def second_product(step):
            b, r = divmod(step, STEPS_PER_BATCH)
            codes, scales = w_codes[step]
            rows = out[b, r * STEP_ROWS : (r + 1) * STEP_ROWS, :].rearrange(
                "(p e) f -> p e f", e=PAIR
            )
            for e in (0, 1):
                acc = banks.tile([P, FEATURES], F32, name="bank", tag="bank")
                for hm in range(HALVES):
                    n_cols = slice((HALVES * e + hm) * P, (HALVES * e + hm + 1) * P)
                    x_codes, x_scales = pos_codes[HALVES * b + hm]
                    nc.tensor.matmul_mx(
                        out=acc[:],
                        lhsT=codes[:, n_cols].bitcast(FP8X4),
                        lhsT_scale=scales[:, n_cols],
                        rhs=x_codes[:].bitcast(FP8X4),
                        rhs_scale=x_scales[:],
                        start=(hm == 0),
                        stop=(hm == HALVES - 1),
                    )
                out_rows = out_pool.tile([P, FEATURES], F32, name="out_rows")
                if step == STEPS - 1:
                    hf = FEATURES // 2
                    nc.scalar.copy(out=out_rows[:, :hf], in_=acc[:, :hf])
                    nc.sync.dma_start(out=rows[:, e, :hf], in_=out_rows[:, :hf])
                    out_rows2 = out_pool.tile([P, hf], F32, name="out_rows2")
                    nc.vector.tensor_copy(out=out_rows2[:], in_=acc[:, hf:])
                    nc.sync.dma_start(out=rows[:, e, hf:], in_=out_rows2[:])
                else:
                    nc.scalar.copy(out=out_rows[:], in_=acc[:])
                    nc.sync.dma_start(out=rows[:, e, :], in_=out_rows[:])

        with tc.manual_schedule():
            load_x(0)
            load_x(1)
            load_v(0, 0)
            load_v(0, 1)
            for r in range(1, STEPS_PER_BATCH):
                load_v(r, 0)
                load_v(r, 1)
                load_x(r + 1)
            for j in range(STEPS_PER_BATCH + 1, HALF_BATCHES):
                load_x(j)

            vcopy = nc.vector.tensor_copy
            scopy = nc.scalar.copy
            for h in range(HALVES):
                for u in range(PAIR):
                    flip_x(h, u)
                regroup_positions(h, vcopy)
            for hm in range(HALVES):
                flip_v(0, hm)
            for h in range(HALVES):
                quantise_features(h)
            for h in range(HALVES):
                quantise_positions(h)
            for step in range(STEPS + 2):
                b, r = divmod(step, STEPS_PER_BATCH)
                nxt = HALVES * (b + 1)
                if step < STEPS:
                    for bank in BANK_ORDER:
                        if bank > 0 or step == 0:
                            fill_bank(step, bank)
                        weigh(step, bank)
                if step + 1 < STEPS:
                    fill_bank(step + 1, 0)
                    copy_for_detour(step + 1, 0)
                if step + 1 < STEPS_PER_BATCH:
                    flip_v(step + 1, 0)
                    flip_v(step + 1, 1)
                if b + 1 < BATCHES and 1 <= r <= 2:
                    flip_x(nxt + r - 1, 0)
                    flip_x(nxt + r - 1, 1)
                if step >= 2:
                    second_product(step - 2)
                if b + 1 < BATCHES:
                    if r in (1, 2) if b == 0 else r == 1:
                        regroup_positions(nxt + r // 2, vcopy, r % 2, 2)
                    else:
                        regroup_positions(nxt + r // 2, scopy, r % 2, 2, run=1)
                if r < 2 and 0 < b < BATCHES:
                    quantise_positions(HALVES * b + r)
                if r >= 2 and b + 1 < BATCHES:
                    quantise_features(nxt + r - 2)
                if step < STEPS:
                    quantise_weighted(step)
